import numpy as np
import ml_dtypes


def mxq(x, axis, fmt="e4m3"):
    dtype, down = {"e4m3": (ml_dtypes.float8_e4m3fn, 7), "e5m2": (ml_dtypes.float8_e5m2, 14)}[fmt]
    v = np.moveaxis(np.asarray(x, np.float32).astype(ml_dtypes.bfloat16).astype(np.float64), axis, -1)
    blocks = v.reshape(v.shape[:-1] + (-1, 32))
    amax = np.abs(blocks).max(-1, keepdims=True)
    byte = np.maximum(np.where(amax > 0, np.frexp(amax)[1] - 1 + 127, 0) - down, 1)
    scale = np.exp2(byte - 127.0)
    codes = (blocks / scale).astype(np.float32).astype(dtype).astype(np.float64)
    return np.moveaxis((codes * scale).reshape(v.shape), -1, axis)


WIDE = False


def mx_kscale(k):
    if not WIDE:
        return np.ones(k)
    levels = np.array([30, -30])
    if k % 512:
        return np.exp2(np.random.permutation(np.resize(levels, k // 32))).repeat(32)
    a = np.empty((k // 512, 16))
    for p in range(k // 512):
        a[p, :8] = np.random.permutation(np.resize(levels, 8))
        for g in range(8):
            far = levels[np.abs(levels - a[p, g]) >= 10]
            a[p, g + 8] = far[np.random.randint(len(far))]
    return np.exp2(a.ravel()).repeat(32)


BF16 = ml_dtypes.bfloat16


def bf(x):
    return np.asarray(x, np.float32).astype(BF16)


def f64(x):
    return np.asarray(x).astype(np.float64)


B, H, L, D = 2, 2, 1024, 1024
NEG = -100.0


def setup_inputs():
    s = mx_kscale(D)
    return {"q": bf(np.random.standard_normal((B, H, L, D)) * s),
            "e": bf(np.random.standard_normal((H, L, D)) / np.sqrt(D) / s)}


def reference(q, e):
    rel = mxq(f64(q), 3, "e5m2") @ mxq(f64(e), 2, "e4m3").transpose(0, 2, 1)
    rel = rel.reshape(B * H, L, L)
    rel = np.pad(rel, ((0, 0), (0, 0), (1, 0)), constant_values=NEG)
    rel = rel.reshape(B * H, L + 1, L)[:, 1:, :][:, :L, :]
    mask = np.triu(np.ones((L, L), dtype=bool), k=1)
    rel = np.where(mask[None, :, :], 0.0, rel)
    return rel.reshape(B, H, L, L)

@@ -1,0 +1,174 @@
+from contextlib import ExitStack
+
+import concourse.mybir as mybir
+from concourse.masks import make_identity
+
+B, H, L, D = 2, 2, 1024, 1024
+FLOPS = B * H * D * L * (L + 1)
+
+F32 = mybir.dt.float32
+BF16 = mybir.dt.bfloat16
+U32 = mybir.dt.uint32
+U8 = mybir.dt.uint8
+E4M3 = mybir.dt.float8_e4m3fn_x4
+E5M2 = mybir.dt.float8_e5m2_x4
+
+P = 128
+PAIR = 2
+BLOCK = P * PAIR
+BLOCKS = L // BLOCK
+PASSES = D // 512
+PITCH = L + 1
+FIRST_LOADS = 16
+LOADS_PER_STORE = 2
+
+
+def tile_subsampledrelativeattention_kernel(tc, q, e, out):
+    nc = tc.nc
+    out_flat = out.rearrange("b h i j -> (b h i j)")
+
+    steps = []
+    for h in range(H):
+        for v in range(BLOCKS):
+            steps.append(("e", h, BLOCKS - 1 - v, None))
+            for b in range(B):
+                steps.append(("q", h, v, b))
+
+    with ExitStack() as ctx:
+        keep = ctx.enter_context(tc.tile_pool(name="keep", bufs=1))
+        ring = ctx.enter_context(tc.tile_pool(name="ring", bufs=3))
+        psum = ctx.enter_context(tc.psum_pool(name="psum", bufs=4))
+        ctx.enter_context(tc.manual_schedule())
+
+        raw = {}
+        grouped = {}
+        codes = {}
+        scales = {}
+        sums = {}
+
+        def load(n):
+            kind, h, v, b = steps[n]
+            rows = e[h] if kind == "e" else q[b, h]
+            raw[n] = keep.tile([P, PAIR * D], BF16, name="raw%d" % n)
+            nc.sync.dma_start(
+                out=raw[n][:],
+                in_=rows[v * BLOCK : (v + 1) * BLOCK, :].rearrange("(p s) k -> p (s k)", s=PAIR),
+            )
+
+        for n in range(FIRST_LOADS):
+            load(n)
+        loaded = FIRST_LOADS
+
+        ident = keep.tile([P, P], F32)
+        make_identity(nc, ident[:])
+        mask = keep.tile([P, PAIR, BLOCK], F32)
+        nc.gpsimd.memset(mask[:], 1.0)
+        for s in range(PAIR):
+            nc.gpsimd.affine_select(
+                out=mask[:, s, :],
+                in_=mask[:, s, :],
+                pattern=[[1, BLOCK]],
+                compare_op=mybir.AluOpType.is_ge,
+                fill=0.0,
+                base=s - (BLOCK - 1),
+                channel_multiplier=PAIR,
+            )
+
+        padded = {}
+        for v in range(BLOCKS):
+            for b in range(B):
+                padded[v, b] = keep.tile([P, PAIR, PITCH], F32, name="padded%d_%d" % (v, b))
+                nc.vector.memset(padded[v, b][:, :, : 2 + L - (v + 1) * BLOCK], 0.0)
+
+        def transpose(n):
+            kind = steps[n][0]
+            words = raw[n][:].bitcast(F32)
+            grouped[n] = ring.tile([P, PAIR * D], BF16, name="grouped", align_bytes=64)
+            for g in range(PASSES):
+                turned = psum.tile([P, PAIR, 2, P], F32, name="turned")
+                for s in range(PAIR):
+                    for u in range(2):
+                        first = s * (D // 2) + g * 256
+                        nc.tensor.transpose(turned[:, s, u, :], words[:, first + u : first + 256 : 2], ident[:])
+                target = grouped[n][:].bitcast(F32)[:, g * 512 : (g + 1) * 512]
+                if kind == "e":
+                    nc.scalar.copy(
+                        out=target.rearrange("p (r w) -> p r w", w=4),
+                        in_=turned[:].rearrange("p s u r -> p r (s u)"),
+                    )
+                else:
+                    nc.scalar.copy(
+                        out=target.rearrange("p (s r u) -> p s r u", s=PAIR, u=2),
+                        in_=turned[:].rearrange("p s u r -> p s r u"),
+                    )
+
+        def quantize(n):
+            kind, h, v, b = steps[n]
+            if kind == "e":
+                key = ("e", h, v)
+                codes[key] = keep.tile([P, PASSES * BLOCK], U32, name="ecodes%d" % n, align_bytes=64)
+                scales[key] = keep.tile([P, PASSES * BLOCK], U8, name="escales%d" % n, align_bytes=64)
+            else:
+                key = n
+                codes[key] = ring.tile([P, PASSES * BLOCK], U32, name="qcodes", align_bytes=64)
+                scales[key] = ring.tile([P, PASSES * BLOCK], U8, name="qscales", align_bytes=64)
+            nc.vector.quantize_mx(
+                out=codes[key][:].bitcast(E4M3 if kind == "e" else E5M2),
+                scales=scales[key][:],
+                in_=grouped[n][:],
+            )
+
+        def multiply(n):
+            kind, h, v, b = steps[n]
+            for j in range(BLOCKS - 1 - v, BLOCKS):
+                acc = psum.tile([P, PAIR, BLOCK], F32, name="acc")
+                for s in range(PAIR):
+                    for g in range(PASSES):
+                        q_cols = slice(g * BLOCK + s * P, g * BLOCK + (s + 1) * P)
+                        e_cols = slice(g * BLOCK, (g + 1) * BLOCK)
+                        nc.tensor.matmul_mx(
+                            out=acc[:, s, :],
+                            lhsT=codes[n][:, q_cols].bitcast(E5M2),
+                            lhsT_scale=scales[n][:, q_cols],
+                            rhs=codes["e", h, j][:, e_cols].bitcast(E4M3),
+                            rhs_scale=scales["e", h, j][:, e_cols],
+                            start=(g == 0),
+                            stop=(g == PASSES - 1),
+                        )
+                target = padded[v, b][:, :, 1 + j * BLOCK : 1 + (j + 1) * BLOCK]
+                if j == BLOCKS - 1 - v:
+                    nc.vector.tensor_tensor(out=target, in0=acc[:], in1=mask[:], op=mybir.AluOpType.mult)
+                elif j == 2:
+                    nc.scalar.copy(out=target, in_=acc[:])
+                else:
+                    nc.vector.tensor_copy(out=target, in_=acc[:])
+
+        def store(n):
+            kind, h, v, b = steps[n]
+            width = PAIR * PITCH
+            source = padded[v, b][:].rearrange("p s x -> p (s x)")
+            start = (b * H + h) * L * L + v * BLOCK * PITCH - L
+            spans = [(0, P)]
+            if v == 0:
+                nc.sync.dma_start(
+                    out=out_flat[start + L : start + width].rearrange("(p x) -> p x", p=1),
+                    in_=source[0:1, L:],
+                )
+                spans = [(1, 113), (113, P)]
+            for lo, hi in spans:
+                nc.sync.dma_start(
+                    out=out_flat[start + lo * width : start + hi * width].rearrange("(p x) -> p x", x=width),
+                    in_=source[lo:hi, :],
+                )
+
+        for n in range(len(steps) + 2):
+            if n < len(steps):
+                transpose(n)
+            if 1 <= n <= len(steps):
+                quantize(n - 1)
+            if n >= 2 and steps[n - 2][0] == "q":
+                multiply(n - 2)
+                store(n - 2)
+                for later in range(loaded, min(loaded + LOADS_PER_STORE, len(steps))):
+                    load(later)
+                loaded = min(loaded + LOADS_PER_STORE, len(steps))

@@ -14,12 +14,14 @@ E4M3 = mybir.dt.float8_e4m3fn_x4
 E5M2 = mybir.dt.float8_e5m2_x4
 
 P = 128
-PAIR = 2
-BLOCK = P * PAIR
+ROWS = 4
+BLOCK = P * ROWS
 BLOCKS = L // BLOCK
-PASSES = D // 512
+K_PASS = 512
+PASSES = D // K_PASS
 PITCH = L + 1
-FIRST_LOADS = 16
+FIRST_LOADS = 8
+HALVED_LOADS = 3
 LOADS_PER_STORE = 2
 
 
@@ -36,7 +38,7 @@ def tile_subsampledrelativeattention_kernel(tc, q, e, out):
 
     with ExitStack() as ctx:
         keep = ctx.enter_context(tc.tile_pool(name="keep", bufs=1))
-        ring = ctx.enter_context(tc.tile_pool(name="ring", bufs=3))
+        ring = ctx.enter_context(tc.tile_pool(name="ring", bufs=2))
         psum = ctx.enter_context(tc.psum_pool(name="psum", bufs=4))
         ctx.enter_context(tc.manual_schedule())
 
@@ -44,16 +46,15 @@ def tile_subsampledrelativeattention_kernel(tc, q, e, out):
         grouped = {}
         codes = {}
         scales = {}
-        sums = {}
 
         def load(n):
             kind, h, v, b = steps[n]
-            rows = e[h] if kind == "e" else q[b, h]
-            raw[n] = keep.tile([P, PAIR * D], BF16, name="raw%d" % n)
-            nc.sync.dma_start(
-                out=raw[n][:],
-                in_=rows[v * BLOCK : (v + 1) * BLOCK, :].rearrange("(p s) k -> p (s k)", s=PAIR),
-            )
+            rows = (e[h] if kind == "e" else q[b, h])[v * BLOCK : (v + 1) * BLOCK, :]
+            rows = rows.rearrange("(p s) k -> p (s k)", s=ROWS)
+            raw[n] = keep.tile([P, ROWS * D], BF16, name="raw%d" % n)
+            piece = ROWS * D // 2 if n < HALVED_LOADS else ROWS * D
+            for c in range(0, ROWS * D, piece):
+                nc.sync.dma_start(out=raw[n][:, c : c + piece], in_=rows[:, c : c + piece])
 
         for n in range(FIRST_LOADS):
             load(n)
@@ -61,114 +62,111 @@ def tile_subsampledrelativeattention_kernel(tc, q, e, out):
 
         ident = keep.tile([P, P], F32)
         make_identity(nc, ident[:])
-        mask = keep.tile([P, PAIR, BLOCK], F32)
+        mask = keep.tile([P, BLOCK + ROWS], F32)
         nc.gpsimd.memset(mask[:], 1.0)
-        for s in range(PAIR):
-            nc.gpsimd.affine_select(
-                out=mask[:, s, :],
-                in_=mask[:, s, :],
-                pattern=[[1, BLOCK]],
-                compare_op=mybir.AluOpType.is_ge,
-                fill=0.0,
-                base=s - (BLOCK - 1),
-                channel_multiplier=PAIR,
-            )
+        nc.gpsimd.affine_select(
+            out=mask[:],
+            in_=mask[:],
+            pattern=[[1, BLOCK + ROWS]],
+            compare_op=mybir.AluOpType.is_ge,
+            fill=0.0,
+            base=1 - BLOCK,
+            channel_multiplier=ROWS,
+        )
 
         padded = {}
         for v in range(BLOCKS):
             for b in range(B):
-                padded[v, b] = keep.tile([P, PAIR, PITCH], F32, name="padded%d_%d" % (v, b))
-                nc.vector.memset(padded[v, b][:, :, : 2 + L - (v + 1) * BLOCK], 0.0)
+                padded[v, b] = keep.tile([P, ROWS, PITCH], F32, name="padded%d_%d" % (v, b))
+                nc.vector.memset(padded[v, b][:, :, : 1 + L - (v + 1) * BLOCK], 0.0)
 
         def transpose(n):
             kind = steps[n][0]
             words = raw[n][:].bitcast(F32)
-            grouped[n] = ring.tile([P, PAIR * D], BF16, name="grouped", align_bytes=64)
-            for g in range(PASSES):
-                turned = psum.tile([P, PAIR, 2, P], F32, name="turned")
-                for s in range(PAIR):
-                    for u in range(2):
-                        first = s * (D // 2) + g * 256
-                        nc.tensor.transpose(turned[:, s, u, :], words[:, first + u : first + 256 : 2], ident[:])
-                target = grouped[n][:].bitcast(F32)[:, g * 512 : (g + 1) * 512]
-                if kind == "e":
-                    nc.scalar.copy(
-                        out=target.rearrange("p (r w) -> p r w", w=4),
-                        in_=turned[:].rearrange("p s u r -> p r (s u)"),
-                    )
-                else:
-                    nc.scalar.copy(
-                        out=target.rearrange("p (s r u) -> p s r u", s=PAIR, u=2),
-                        in_=turned[:].rearrange("p s u r -> p s r u"),
-                    )
+            grouped[n] = ring.tile([P, PASSES, BLOCK * 4], BF16, name="grouped", align_bytes=64)
+            for s0 in range(0, ROWS, 2):
+                for g in range(PASSES):
+                    turned = psum.tile([P, 2, 2, P], F32, name="turned")
+                    for s in range(2):
+                        for u in range(2):
+                            first = (s0 + s) * (D // 2) + g * (K_PASS // 2)
+                            nc.tensor.transpose(
+                                turned[:, s, u, :], words[:, first + u : first + K_PASS // 2 : 2], ident[:]
+                            )
+                    target = grouped[n][:, g, :].bitcast(F32)
+                    if kind == "e":
+                        nc.scalar.copy(
+                            out=target.rearrange("p (r w) -> p r w", r=P)[:, :, 2 * s0 : 2 * s0 + 4],
+                            in_=turned[:].rearrange("p s u r -> p r (s u)"),
+                        )
+                    else:
+                        nc.scalar.copy(
+                            out=target.rearrange("p (s r u) -> p s r u", s=ROWS, u=2)[:, s0 : s0 + 2],
+                            in_=turned[:].rearrange("p s u r -> p s r u"),
+                        )
 
         def quantize(n):
             kind, h, v, b = steps[n]
             if kind == "e":
                 key = ("e", h, v)
-                codes[key] = keep.tile([P, PASSES * BLOCK], U32, name="ecodes%d" % n, align_bytes=64)
-                scales[key] = keep.tile([P, PASSES * BLOCK], U8, name="escales%d" % n, align_bytes=64)
+                codes[key] = keep.tile([P, PASSES, BLOCK], U32, name="ecodes%d" % n, align_bytes=64)
+                scales[key] = keep.tile([P, PASSES, BLOCK], U8, name="escales%d" % n, align_bytes=64)
             else:
                 key = n
-                codes[key] = ring.tile([P, PASSES * BLOCK], U32, name="qcodes", align_bytes=64)
-                scales[key] = ring.tile([P, PASSES * BLOCK], U8, name="qscales", align_bytes=64)
-            nc.vector.quantize_mx(
-                out=codes[key][:].bitcast(E4M3 if kind == "e" else E5M2),
-                scales=scales[key][:],
-                in_=grouped[n][:],
-            )
+                codes[key] = ring.tile([P, PASSES, BLOCK], U32, name="qcodes", align_bytes=64)
+                scales[key] = ring.tile([P, PASSES, BLOCK], U8, name="qscales", align_bytes=64)
+            for g in range(PASSES):
+                nc.vector.quantize_mx(
+                    out=codes[key][:, g, :].bitcast(E4M3 if kind == "e" else E5M2),
+                    scales=scales[key][:, g, :],
+                    in_=grouped[n][:, g, :],
+                )
 
         def multiply(n):
             kind, h, v, b = steps[n]
-            for j in range(BLOCKS - 1 - v, BLOCKS):
-                acc = psum.tile([P, PAIR, BLOCK], F32, name="acc")
-                for s in range(PAIR):
+            for s in range(ROWS):
+                for j in range(BLOCKS - 1 - v, BLOCKS):
+                    acc = psum.tile([P, BLOCK], F32, name="acc")
                     for g in range(PASSES):
-                        q_cols = slice(g * BLOCK + s * P, g * BLOCK + (s + 1) * P)
-                        e_cols = slice(g * BLOCK, (g + 1) * BLOCK)
                         nc.tensor.matmul_mx(
-                            out=acc[:, s, :],
-                            lhsT=codes[n][:, q_cols].bitcast(E5M2),
-                            lhsT_scale=scales[n][:, q_cols],
-                            rhs=codes["e", h, j][:, e_cols].bitcast(E4M3),
-                            rhs_scale=scales["e", h, j][:, e_cols],
+                            out=acc[:],
+                            lhsT=codes[n][:, g, s * P : (s + 1) * P].bitcast(E5M2),
+                            lhsT_scale=scales[n][:, g, s * P : (s + 1) * P],
+                            rhs=codes["e", h, j][:, g, :].bitcast(E4M3),
+                            rhs_scale=scales["e", h, j][:, g, :],
                             start=(g == 0),
                             stop=(g == PASSES - 1),
                         )
-                target = padded[v, b][:, :, 1 + j * BLOCK : 1 + (j + 1) * BLOCK]
-                if j == BLOCKS - 1 - v:
-                    nc.vector.tensor_tensor(out=target, in0=acc[:], in1=mask[:], op=mybir.AluOpType.mult)
-                elif j == 2:
-                    nc.scalar.copy(out=target, in_=acc[:])
-                else:
-                    nc.vector.tensor_copy(out=target, in_=acc[:])
+                    target = padded[v, b][:, s, 1 + j * BLOCK : 1 + (j + 1) * BLOCK]
+                    if j == BLOCKS - 1 - v:
+                        nc.vector.tensor_tensor(
+                            out=target, in0=acc[:], in1=mask[:, s : s + BLOCK], op=mybir.AluOpType.mult
+                        )
+                    else:
+                        nc.scalar.copy(out=target, in_=acc[:])
 
         def store(n):
             kind, h, v, b = steps[n]
-            width = PAIR * PITCH
+            width = ROWS * PITCH
             source = padded[v, b][:].rearrange("p s x -> p (s x)")
             start = (b * H + h) * L * L + v * BLOCK * PITCH - L
-            spans = [(0, P)]
-            if v == 0:
-                nc.sync.dma_start(
-                    out=out_flat[start + L : start + width].rearrange("(p x) -> p x", p=1),
-                    in_=source[0:1, L:],
-                )
-                spans = [(1, 113), (113, P)]
-            for lo, hi in spans:
-                nc.sync.dma_start(
-                    out=out_flat[start + lo * width : start + hi * width].rearrange("(p x) -> p x", x=width),
-                    in_=source[lo:hi, :],
-                )
+            if v > 0:
+                rows = out_flat[start : start + P * width].rearrange("(p x) -> p x", x=width)
+                nc.sync.dma_start(out=rows, in_=source)
+            else:
+                rows = out_flat[start + L : start + L + P * width].rearrange("(p x) -> p x", x=width)
+                nc.sync.dma_start(out=rows[:, : width - L], in_=source[:, L:])
+                for lo, hi in ((1, 113), (113, P)):
+                    nc.gpsimd.dma_start(out=rows[lo - 1 : hi - 1, width - L :], in_=source[lo:hi, :L])
 
-        for n in range(len(steps) + 2):
+        for n in range(len(steps) + 1):
             if n < len(steps):
                 transpose(n)
-            if 1 <= n <= len(steps):
-                quantize(n - 1)
-            if n >= 2 and steps[n - 2][0] == "q":
-                multiply(n - 2)
-                store(n - 2)
+            if n >= 1 and steps[n - 1][0] == "q":
+                multiply(n - 1)
+                store(n - 1)
                 for later in range(loaded, min(loaded + LOADS_PER_STORE, len(steps))):
                     load(later)
                 loaded = min(loaded + LOADS_PER_STORE, len(steps))
+            if n < len(steps):
+                quantize(n)

@@ -23,6 +23,8 @@ PITCH = L + 1
 FIRST_LOADS = 8
 HALVED_LOADS = 3
 LOADS_PER_STORE = 2
+RAW_BUFS = 10
+BANKS_PER_STEP = 4
 
 
 def tile_subsampledrelativeattention_kernel(tc, q, e, out):
@@ -43,6 +45,7 @@ def tile_subsampledrelativeattention_kernel(tc, q, e, out):
         ctx.enter_context(tc.manual_schedule())
 
         raw = {}
+        shuffled = {}
         grouped = {}
         codes = {}
         scales = {}
@@ -51,7 +54,7 @@ def tile_subsampledrelativeattention_kernel(tc, q, e, out):
             kind, h, v, b = steps[n]
             rows = (e[h] if kind == "e" else q[b, h])[v * BLOCK : (v + 1) * BLOCK, :]
             rows = rows.rearrange("(p s) k -> p (s k)", s=ROWS)
-            raw[n] = keep.tile([P, ROWS * D], BF16, name="raw%d" % n)
+            raw[n] = ring.tile([P, ROWS * D], BF16, name="raw", bufs=RAW_BUFS)
             piece = ROWS * D // 2 if n < HALVED_LOADS else ROWS * D
             for c in range(0, ROWS * D, piece):
                 nc.sync.dma_start(out=raw[n][:, c : c + piece], in_=rows[:, c : c + piece])
@@ -75,24 +78,33 @@ def tile_subsampledrelativeattention_kernel(tc, q, e, out):
         )
 
         padded = {}
-        for v in range(BLOCKS):
-            for b in range(B):
+
+        def zero(b):
+            for v in range(BLOCKS):
                 padded[v, b] = keep.tile([P, ROWS, PITCH], F32, name="padded%d_%d" % (v, b))
-                nc.vector.memset(padded[v, b][:, :, : 1 + L - (v + 1) * BLOCK], 0.0)
+                pairs = padded[v, b][:].rearrange("p (a c) x -> p a (c x)", c=2)[:, :, : 2 * L]
+                nc.vector.memset(pairs.rearrange("p a (c x) -> p a c x", c=2)[:, :, :, : 2 + L - (v + 1) * BLOCK], 0.0)
+
+        def shuffle(n, share_with_scalar):
+            for s0 in range(0, ROWS, 2):
+                shuffled[n, s0] = ring.tile([P, 2 * D], BF16, name="shuffled", bufs=3)
+                target = shuffled[n, s0][:].rearrange("p (u x a) -> p u x a", u=2, a=16)
+                source = raw[n][:, s0 * D : (s0 + 2) * D].rearrange("p (x u a) -> p u x a", u=2, a=16)
+                if s0 > 0 and share_with_scalar:
+                    nc.scalar.copy(out=target, in_=source)
+                else:
+                    nc.vector.tensor_copy(out=target, in_=source)
 
         def transpose(n):
             kind = steps[n][0]
-            words = raw[n][:].bitcast(F32)
             grouped[n] = ring.tile([P, PASSES, BLOCK * 4], BF16, name="grouped", align_bytes=64)
             for s0 in range(0, ROWS, 2):
+                words = shuffled[n, s0][:].bitcast(F32).rearrange("p (u s g w) -> p u s g w", u=2, s=2, g=PASSES)
                 for g in range(PASSES):
                     turned = psum.tile([P, 2, 2, P], F32, name="turned")
                     for s in range(2):
                         for u in range(2):
-                            first = (s0 + s) * (D // 2) + g * (K_PASS // 2)
-                            nc.tensor.transpose(
-                                turned[:, s, u, :], words[:, first + u : first + K_PASS // 2 : 2], ident[:]
-                            )
+                            nc.tensor.transpose(turned[:, s, u, :], words[:, u, s, g, :], ident[:])
                     target = grouped[n][:, g, :].bitcast(F32)
                     if kind == "e":
                         nc.scalar.copy(
@@ -113,8 +125,8 @@ def tile_subsampledrelativeattention_kernel(tc, q, e, out):
                 scales[key] = keep.tile([P, PASSES, BLOCK], U8, name="escales%d" % n, align_bytes=64)
             else:
                 key = n
-                codes[key] = ring.tile([P, PASSES, BLOCK], U32, name="qcodes", align_bytes=64)
-                scales[key] = ring.tile([P, PASSES, BLOCK], U8, name="qscales", align_bytes=64)
+                codes[key] = ring.tile([P, PASSES, BLOCK], U32, name="qcodes", bufs=4, align_bytes=64)
+                scales[key] = ring.tile([P, PASSES, BLOCK], U8, name="qscales", bufs=4, align_bytes=64)
             for g in range(PASSES):
                 nc.vector.quantize_mx(
                     out=codes[key][:, g, :].bitcast(E4M3 if kind == "e" else E5M2),
@@ -122,28 +134,24 @@ def tile_subsampledrelativeattention_kernel(tc, q, e, out):
                     in_=grouped[n][:, g, :],
                 )
 
-        def multiply(n):
+        def multiply(n, s, j):
             kind, h, v, b = steps[n]
-            for s in range(ROWS):
-                for j in range(BLOCKS - 1 - v, BLOCKS):
-                    acc = psum.tile([P, BLOCK], F32, name="acc")
-                    for g in range(PASSES):
-                        nc.tensor.matmul_mx(
-                            out=acc[:],
-                            lhsT=codes[n][:, g, s * P : (s + 1) * P].bitcast(E5M2),
-                            lhsT_scale=scales[n][:, g, s * P : (s + 1) * P],
-                            rhs=codes["e", h, j][:, g, :].bitcast(E4M3),
-                            rhs_scale=scales["e", h, j][:, g, :],
-                            start=(g == 0),
-                            stop=(g == PASSES - 1),
-                        )
-                    target = padded[v, b][:, s, 1 + j * BLOCK : 1 + (j + 1) * BLOCK]
-                    if j == BLOCKS - 1 - v:
-                        nc.vector.tensor_tensor(
-                            out=target, in0=acc[:], in1=mask[:, s : s + BLOCK], op=mybir.AluOpType.mult
-                        )
-                    else:
-                        nc.scalar.copy(out=target, in_=acc[:])
+            acc = psum.tile([P, BLOCK], F32, name="acc")
+            for g in range(PASSES):
+                nc.tensor.matmul_mx(
+                    out=acc[:],
+                    lhsT=codes[n][:, g, s * P : (s + 1) * P].bitcast(E5M2),
+                    lhsT_scale=scales[n][:, g, s * P : (s + 1) * P],
+                    rhs=codes["e", h, j][:, g, :].bitcast(E4M3),
+                    rhs_scale=scales["e", h, j][:, g, :],
+                    start=(g == 0),
+                    stop=(g == PASSES - 1),
+                )
+            target = padded[v, b][:, s, 1 + j * BLOCK : 1 + (j + 1) * BLOCK]
+            if j == BLOCKS - 1 - v:
+                nc.vector.tensor_tensor(out=target, in0=acc[:], in1=mask[:, s : s + BLOCK], op=mybir.AluOpType.mult)
+            else:
+                nc.scalar.copy(out=target, in_=acc[:])
 
         def store(n):
             kind, h, v, b = steps[n]
@@ -159,14 +167,29 @@ def tile_subsampledrelativeattention_kernel(tc, q, e, out):
                 for lo, hi in ((1, 113), (113, P)):
                     nc.gpsimd.dma_start(out=rows[lo - 1 : hi - 1, width - L :], in_=source[lo:hi, :L])
 
-        for n in range(len(steps) + 1):
+        waiting = []
+        zero(0)
+        shuffle(0, False)
+        zero(1)
+        n = 0
+        while n < len(steps) or waiting:
+            now = waiting[:BANKS_PER_STEP]
+            waiting = waiting[BANKS_PER_STEP:]
             if n < len(steps):
                 transpose(n)
-            if n >= 1 and steps[n - 1][0] == "q":
-                multiply(n - 1)
-                store(n - 1)
-                for later in range(loaded, min(loaded + LOADS_PER_STORE, len(steps))):
-                    load(later)
-                loaded = min(loaded + LOADS_PER_STORE, len(steps))
+            if n + 1 < len(steps):
+                all_masked = len(now) > 0 and all(steps[m][2] == 0 for m, s, j in now)
+                shuffle(n + 1, all_masked)
+            for m, s, j in now:
+                multiply(m, s, j)
+                if s == ROWS - 1 and j == BLOCKS - 1:
+                    store(m)
+                    for later in range(loaded, min(loaded + LOADS_PER_STORE, len(steps))):
+                        load(later)
+                    loaded = min(loaded + LOADS_PER_STORE, len(steps))
             if n < len(steps):
                 quantize(n)
+                if steps[n][0] == "q":
+                    v = steps[n][2]
+                    waiting += [(n, s, j) for s in range(ROWS) for j in range(BLOCKS - 1 - v, BLOCKS)]
+            n += 1

from contextlib import ExitStack

import concourse.mybir as mybir
from concourse.masks import make_identity

B, H, L, D = 2, 2, 1024, 1024
FLOPS = B * H * D * L * (L + 1)

F32 = mybir.dt.float32
BF16 = mybir.dt.bfloat16
U32 = mybir.dt.uint32
U8 = mybir.dt.uint8
E4M3 = mybir.dt.float8_e4m3fn_x4
E5M2 = mybir.dt.float8_e5m2_x4

P = 128
ROWS = 4
BLOCK = P * ROWS
BLOCKS = L // BLOCK
K_PASS = 512
PASSES = D // K_PASS
PITCH = L + 1
FIRST_LOADS = 8
HALVED_LOADS = 3
LOADS_PER_STORE = 2
RAW_BUFS = 10
BANKS_PER_STEP = 4


def tile_subsampledrelativeattention_kernel(tc, q, e, out):
    nc = tc.nc
    out_flat = out.rearrange("b h i j -> (b h i j)")

    steps = []
    for h in range(H):
        for v in range(BLOCKS):
            steps.append(("e", h, BLOCKS - 1 - v, None))
            for b in range(B):
                steps.append(("q", h, v, b))

    with ExitStack() as ctx:
        keep = ctx.enter_context(tc.tile_pool(name="keep", bufs=1))
        ring = ctx.enter_context(tc.tile_pool(name="ring", bufs=2))
        psum = ctx.enter_context(tc.psum_pool(name="psum", bufs=4))
        ctx.enter_context(tc.manual_schedule())

        raw = {}
        shuffled = {}
        grouped = {}
        codes = {}
        scales = {}

        def load(n):
            kind, h, v, b = steps[n]
            rows = (e[h] if kind == "e" else q[b, h])[v * BLOCK : (v + 1) * BLOCK, :]
            rows = rows.rearrange("(p s) k -> p (s k)", s=ROWS)
            raw[n] = ring.tile([P, ROWS * D], BF16, name="raw", bufs=RAW_BUFS)
            piece = ROWS * D // 2 if n < HALVED_LOADS else ROWS * D
            for c in range(0, ROWS * D, piece):
                nc.sync.dma_start(out=raw[n][:, c : c + piece], in_=rows[:, c : c + piece])

        for n in range(FIRST_LOADS):
            load(n)
        loaded = FIRST_LOADS

        ident = keep.tile([P, P], F32)
        make_identity(nc, ident[:])
        mask = keep.tile([P, BLOCK + ROWS], F32)
        nc.gpsimd.memset(mask[:], 1.0)
        nc.gpsimd.affine_select(
            out=mask[:],
            in_=mask[:],
            pattern=[[1, BLOCK + ROWS]],
            compare_op=mybir.AluOpType.is_ge,
            fill=0.0,
            base=1 - BLOCK,
            channel_multiplier=ROWS,
        )

        padded = {}

        def zero(b):
            for v in range(BLOCKS):
                padded[v, b] = keep.tile([P, ROWS, PITCH], F32, name="padded%d_%d" % (v, b))
                pairs = padded[v, b][:].rearrange("p (a c) x -> p a (c x)", c=2)[:, :, : 2 * L]
                nc.vector.memset(pairs.rearrange("p a (c x) -> p a c x", c=2)[:, :, :, : 2 + L - (v + 1) * BLOCK], 0.0)

        def shuffle(n, share_with_scalar):
            for s0 in range(0, ROWS, 2):
                shuffled[n, s0] = ring.tile([P, 2 * D], BF16, name="shuffled", bufs=3)
                target = shuffled[n, s0][:].rearrange("p (u x a) -> p u x a", u=2, a=16)
                source = raw[n][:, s0 * D : (s0 + 2) * D].rearrange("p (x u a) -> p u x a", u=2, a=16)
                if s0 > 0 and share_with_scalar:
                    nc.scalar.copy(out=target, in_=source)
                else:
                    nc.vector.tensor_copy(out=target, in_=source)

        def transpose(n):
            kind = steps[n][0]
            grouped[n] = ring.tile([P, PASSES, BLOCK * 4], BF16, name="grouped", align_bytes=64)
            for s0 in range(0, ROWS, 2):
                words = shuffled[n, s0][:].bitcast(F32).rearrange("p (u s g w) -> p u s g w", u=2, s=2, g=PASSES)
                for g in range(PASSES):
                    turned = psum.tile([P, 2, 2, P], F32, name="turned")
                    for s in range(2):
                        for u in range(2):
                            nc.tensor.transpose(turned[:, s, u, :], words[:, u, s, g, :], ident[:])
                    target = grouped[n][:, g, :].bitcast(F32)
                    if kind == "e":
                        nc.scalar.copy(
                            out=target.rearrange("p (r w) -> p r w", r=P)[:, :, 2 * s0 : 2 * s0 + 4],
                            in_=turned[:].rearrange("p s u r -> p r (s u)"),
                        )
                    else:
                        nc.scalar.copy(
                            out=target.rearrange("p (s r u) -> p s r u", s=ROWS, u=2)[:, s0 : s0 + 2],
                            in_=turned[:].rearrange("p s u r -> p s r u"),
                        )

        def quantize(n):
            kind, h, v, b = steps[n]
            if kind == "e":
                key = ("e", h, v)
                codes[key] = keep.tile([P, PASSES, BLOCK], U32, name="ecodes%d" % n, align_bytes=64)
                scales[key] = keep.tile([P, PASSES, BLOCK], U8, name="escales%d" % n, align_bytes=64)
            else:
                key = n
                codes[key] = ring.tile([P, PASSES, BLOCK], U32, name="qcodes", bufs=4, align_bytes=64)
                scales[key] = ring.tile([P, PASSES, BLOCK], U8, name="qscales", bufs=4, align_bytes=64)
            for g in range(PASSES):
                nc.vector.quantize_mx(
                    out=codes[key][:, g, :].bitcast(E4M3 if kind == "e" else E5M2),
                    scales=scales[key][:, g, :],
                    in_=grouped[n][:, g, :],
                )

        def multiply(n, s, j):
            kind, h, v, b = steps[n]
            acc = psum.tile([P, BLOCK], F32, name="acc")
            for g in range(PASSES):
                nc.tensor.matmul_mx(
                    out=acc[:],
                    lhsT=codes[n][:, g, s * P : (s + 1) * P].bitcast(E5M2),
                    lhsT_scale=scales[n][:, g, s * P : (s + 1) * P],
                    rhs=codes["e", h, j][:, g, :].bitcast(E4M3),
                    rhs_scale=scales["e", h, j][:, g, :],
                    start=(g == 0),
                    stop=(g == PASSES - 1),
                )
            target = padded[v, b][:, s, 1 + j * BLOCK : 1 + (j + 1) * BLOCK]
            if j == BLOCKS - 1 - v:
                nc.vector.tensor_tensor(out=target, in0=acc[:], in1=mask[:, s : s + BLOCK], op=mybir.AluOpType.mult)
            else:
                nc.scalar.copy(out=target, in_=acc[:])

        def store(n):
            kind, h, v, b = steps[n]
            width = ROWS * PITCH
            source = padded[v, b][:].rearrange("p s x -> p (s x)")
            start = (b * H + h) * L * L + v * BLOCK * PITCH - L
            if v > 0:
                rows = out_flat[start : start + P * width].rearrange("(p x) -> p x", x=width)
                nc.sync.dma_start(out=rows, in_=source)
            else:
                rows = out_flat[start + L : start + L + P * width].rearrange("(p x) -> p x", x=width)
                nc.sync.dma_start(out=rows[:, : width - L], in_=source[:, L:])
                for lo, hi in ((1, 113), (113, P)):
                    nc.gpsimd.dma_start(out=rows[lo - 1 : hi - 1, width - L :], in_=source[lo:hi, :L])

        waiting = []
        zero(0)
        shuffle(0, False)
        zero(1)
        n = 0
        while n < len(steps) or waiting:
            now = waiting[:BANKS_PER_STEP]
            waiting = waiting[BANKS_PER_STEP:]
            if n < len(steps):
                transpose(n)
            if n + 1 < len(steps):
                all_masked = len(now) > 0 and all(steps[m][2] == 0 for m, s, j in now)
                shuffle(n + 1, all_masked)
            for m, s, j in now:
                multiply(m, s, j)
                if s == ROWS - 1 and j == BLOCKS - 1:
                    store(m)
                    for later in range(loaded, min(loaded + LOADS_PER_STORE, len(steps))):
                        load(later)
                    loaded = min(loaded + LOADS_PER_STORE, len(steps))
            if n < len(steps):
                quantize(n)
                if steps[n][0] == "q":
                    v = steps[n][2]
                    waiting += [(n, s, j) for s in range(ROWS) for j in range(BLOCKS - 1 - v, BLOCKS)]
            n += 1
